import numpy as np
import ml_dtypes


def mxq(x, axis, fmt="e4m3"):
    dtype, down = {"e4m3": (ml_dtypes.float8_e4m3fn, 7), "e5m2": (ml_dtypes.float8_e5m2, 14)}[fmt]
    v = np.moveaxis(np.asarray(x, np.float32).astype(ml_dtypes.bfloat16).astype(np.float64), axis, -1)
    blocks = v.reshape(v.shape[:-1] + (-1, 32))
    amax = np.abs(blocks).max(-1, keepdims=True)
    byte = np.maximum(np.where(amax > 0, np.frexp(amax)[1] - 1 + 127, 0) - down, 1)
    scale = np.exp2(byte - 127.0)
    codes = (blocks / scale).astype(np.float32).astype(dtype).astype(np.float64)
    return np.moveaxis((codes * scale).reshape(v.shape), -1, axis)


WIDE = False


def mx_kscale(k):
    if not WIDE:
        return np.ones(k)
    levels = np.array([30, -30])
    if k % 512:
        return np.exp2(np.random.permutation(np.resize(levels, k // 32))).repeat(32)
    a = np.empty((k // 512, 16))
    for p in range(k // 512):
        a[p, :8] = np.random.permutation(np.resize(levels, 8))
        for g in range(8):
            far = levels[np.abs(levels - a[p, g]) >= 10]
            a[p, g + 8] = far[np.random.randint(len(far))]
    return np.exp2(a.ravel()).repeat(32)


BF16 = ml_dtypes.bfloat16


def bf(x):
    return np.asarray(x, np.float32).astype(BF16)


def f64(x):
    return np.asarray(x).astype(np.float64)


B, S, E, H, D = 1, 512, 2048, 16, 128
ROPE_BASE = 10000.0
HALF = D // 2


def rope_interleaved(t):
    inv_freq = 1.0 / (ROPE_BASE ** (np.arange(HALF) * 2.0 / D))
    ang = np.arange(S)[:, None] * inv_freq[None, :]
    cos = np.cos(ang)[None, :, None, :]
    sin = np.sin(ang)[None, :, None, :]
    t0 = t[..., 0::2]
    t1 = t[..., 1::2]
    out = np.stack([t0 * cos - t1 * sin, t1 * cos + t0 * sin], axis=-1)
    return out.reshape(B, S, H, D)


def setup_inputs():
    s = mx_kscale(E)
    return {"x": bf(np.random.standard_normal((B, S, E)) * s),
            "Wq": bf(np.random.standard_normal((E, H * D)) / np.sqrt(E) / s[:, None]),
            "Wk": bf(np.random.standard_normal((E, H * D)) / np.sqrt(E) / s[:, None])}


def reference(x, Wq, Wk):
    xq = mxq(f64(x), 2, "e5m2")
    q = (xq @ mxq(f64(Wq), 0, "e5m2")).reshape(B, S, H, D)
    k = (xq @ mxq(f64(Wk), 0, "e5m2")).reshape(B, S, H, D)
    q = rope_interleaved(q)
    k = rope_interleaved(k)
    return q.transpose(0, 2, 1, 3), k.transpose(0, 2, 1, 3)

@@ -1,0 +1,206 @@
+from contextlib import ExitStack
+import math
+
+import concourse.mybir as mybir
+from concourse.masks import make_identity
+
+F32 = mybir.dt.float32
+BF16 = mybir.dt.bfloat16
+U32 = mybir.dt.uint32
+U8 = mybir.dt.uint8
+I32 = mybir.dt.int32
+E5X4 = mybir.dt.float8_e5m2_x4
+ALU = mybir.AluOpType
+ACT = mybir.ActivationFunctionType
+
+P = 128
+FLOPS = 2 * 512 * 2048 * 4096
+
+V_UNITS = (1, 3, 5)
+RAW_BUFS = 10
+RATE = 1.15
+
+
+def tile_multiheadselfattention_pa_kernel(tc, x, Wq, Wk, out_0, out_1):
+    nc = tc.nc
+    mats = (Wq, Wk)
+    outs = (out_0, out_1)
+
+    with ExitStack() as ctx:
+        cst = ctx.enter_context(tc.tile_pool(name="cst", bufs=1))
+        rawp = ctx.enter_context(tc.tile_pool(name="rawp", bufs=RAW_BUFS))
+        xrp = ctx.enter_context(tc.tile_pool(name="xrp", bufs=4))
+        gxp = ctx.enter_context(tc.tile_pool(name="gxp", bufs=2))
+        gwp = ctx.enter_context(tc.tile_pool(name="gwp", bufs=6))
+        cdp = ctx.enter_context(tc.tile_pool(name="cdp", bufs=3))
+        abp = ctx.enter_context(tc.tile_pool(name="abp", bufs=3))
+        rp = ctx.enter_context(tc.tile_pool(name="rp", bufs=3))
+        psx = ctx.enter_context(tc.psum_pool(name="psx", bufs=2))
+        psm = ctx.enter_context(tc.psum_pool(name="psm", bufs=6))
+
+        raw = {}
+        xraw = {}
+
+        def load_w(mat, hf, g):
+            t = rawp.tile([P, 4, 1024], BF16, name="wraw", tag="wraw")
+            nc.sync.dma_start(
+                out=t[:],
+                in_=mats[mat][512 * g:512 * (g + 1), 1024 * hf:1024 * (hf + 1)].rearrange("(p j) w -> p j w", j=4),
+            )
+            raw[(mat, hf, g)] = t
+
+        def load_x(g):
+            t = xrp.tile([P, 4, 512], BF16, name="xraw", tag="xraw")
+            nc.sync.dma_start(out=t[:], in_=x[0, :, 512 * g:512 * (g + 1)].rearrange("(m a) k -> m a k", a=4))
+            xraw[g] = t
+
+        for g in range(4):
+            load_w(0, 0, g)
+            load_x(g)
+        for mat, hf in ((0, 1), (1, 0), (1, 1)):
+            for g in range(4):
+                load_w(mat, hf, g)
+
+        ident = cst.tile([P, P], F32, name="ident")
+        make_identity(nc, ident[:])
+        pos = cst.tile([P, 4], F32, name="pos")
+        nc.gpsimd.iota(pos[:], pattern=[[1, 4]], base=0, channel_multiplier=4, allow_small_or_imprecise_dtypes=True)
+        ones = cst.tile([P, 8], F32, name="ones")
+        nc.vector.memset(ones[:], 1.0)
+        t0 = cst.tile([P, 8, 8], F32, name="t0")
+        t1 = cst.tile([P, 8, 8], F32, name="t1")
+        for k in range(8):
+            nc.vector.tensor_scalar(out=t0[:, :, k], in0=ones[:], scalar1=10000.0 ** (-k / 64.0) / (2.0 * math.pi),
+                                    scalar2=None, op0=ALU.mult)
+            nc.vector.tensor_scalar(out=t1[:, k, :], in0=ones[:], scalar1=10000.0 ** (-8.0 * k / 64.0),
+                                    scalar2=None, op0=ALU.mult)
+        frq = cst.tile([P, 64], F32, name="frq")
+        nc.vector.tensor_tensor(out=frq[:], in0=t0[:].rearrange("p a b -> p (a b)"),
+                                in1=t1[:].rearrange("p a b -> p (a b)"), op=ALU.mult)
+        turns = cst.tile([P, 2, 4, 64], F32, name="turns")
+        for a in range(4):
+            nc.vector.tensor_scalar(out=turns[:, 0, a, :], in0=frq[:], scalar1=pos[:, a:a + 1], scalar2=None,
+                                    op0=ALU.mult)
+        nc.vector.tensor_scalar(out=turns[:, 1], in0=turns[:, 0], scalar1=0.25, scalar2=None, op0=ALU.add)
+        whole = cst.tile([P, 2, 4, 64], I32, name="whole")
+        nc.vector.tensor_copy(out=whole[:], in_=turns[:])
+        frac = cst.tile([P, 2, 4, 64], F32, name="frac")
+        nc.vector.tensor_tensor(out=frac[:], in0=turns[:], in1=whole[:], op=ALU.subtract)
+        nfrac = cst.tile([P, 2, 4, 64], F32, name="nfrac")
+        nc.vector.scalar_tensor_tensor(out=nfrac[:], in0=frac[:], scalar=0.5, in1=frac[:], op0=ALU.is_ge,
+                                       op1=ALU.subtract)
+        cosT = cst.tile([P, 4, 64, 2], F32, name="cosT")
+        sinT = cst.tile([P, 4, 64, 2], F32, name="sinT")
+        nc.scalar.activation(out=cosT[:], in_=nfrac[:, 1].unsqueeze(3).to_broadcast([P, 4, 64, 2]), func=ACT.Sin,
+                             scale=-2.0 * math.pi)
+        nc.scalar.activation(out=sinT[:, :, :, 0], in_=nfrac[:, 0], func=ACT.Sin, scale=-2.0 * math.pi)
+        nc.scalar.activation(out=sinT[:, :, :, 1], in_=nfrac[:, 0], func=ACT.Sin, scale=2.0 * math.pi)
+
+        xq = cst.tile([P, 4, 4, 128], U32, name="xq", align_bytes=64)
+        xsc = cst.tile([P, 4, 4, 128], U8, name="xsc", align_bytes=64)
+        for g in range(4):
+            xw = xraw[g][:].rearrange("p a k -> p (a k)").bitcast(F32)
+            gx = gxp.tile([P, 4, 128, 2], F32, name="gx", tag="gx", align_bytes=64)
+            for h2 in range(2):
+                xt = psx.tile([P, 2, 2, 128], F32, name="xt", tag="xt")
+                for a2 in range(2):
+                    a = 2 * h2 + a2
+                    for u in range(2):
+                        nc.tensor.transpose(out=xt[:, a2, u, :], in_=xw[:, 256 * a + u:256 * (a + 1):2],
+                                            identity=ident[:])
+                nc.scalar.copy(out=gx[:, 2 * h2:2 * h2 + 2], in_=xt[:].rearrange("p a u m -> p a m u"))
+            nc.vector.quantize_mx(
+                out=xq[:, g].rearrange("p a m -> p (a m)").bitcast(E5X4),
+                scales=xsc[:, g].rearrange("p a m -> p (a m)"),
+                in_=gx[:].rearrange("p a m u -> p (a m u)").bitcast(BF16),
+            )
+
+        units = []
+        for g in range(4):
+            units.extend([(0, g), (1, g)])
+        for c in range(2, 8):
+            units.extend([(c, g) for g in range(4)])
+        last_unit = {}
+        for s, (c, g) in enumerate(units):
+            last_unit[c] = s
+        tiles = [(c, a) for c in range(8) for a in range(4)]
+
+        codes = {}
+        grouped = {}
+        rout = {}
+        pend = []
+
+        def interleave(s):
+            c, g = units[s]
+            src = raw[(c // 4, (c % 4) // 2, g)]
+            w0 = 512 * (c % 2)
+            gw = gwp.tile([P, 512, 4], BF16, name="gw", tag="gw", align_bytes=64)
+            view = src[:, :, w0:w0 + 512].rearrange("p j w -> p w j")
+            if s in V_UNITS:
+                nc.vector.tensor_copy(out=gw[:], in_=view)
+            else:
+                nc.scalar.copy(out=gw[:], in_=view)
+            grouped[s] = gw
+
+        def quantise(s):
+            c, g = units[s]
+            if c not in codes:
+                wc = cdp.tile([P, 4, 512], U32, name="wc", tag="wc", align_bytes=64)
+                ws = cdp.tile([P, 4, 512], U8, name="ws", tag="ws", align_bytes=64)
+                codes[c] = (wc, ws)
+            wc, ws = codes[c]
+            nc.vector.quantize_mx(out=wc[:, g, :].bitcast(E5X4), scales=ws[:, g, :],
+                                  in_=grouped[s][:].rearrange("p w j -> p (w j)"))
+
+        def finish(c, a, pa, pb):
+            r = rout[c]
+            nc.vector.tensor_tensor(
+                out=r[:, :, a, :].rearrange("p h (i e) -> p h i e", e=2),
+                in0=pa[:].rearrange("p (h i e) -> p h i e", h=4, e=2),
+                in1=pb[:].rearrange("p (h i e) -> p h i e", h=4, e=2)[:, :, :, ::-1],
+                op=ALU.add,
+            )
+            if a == 3:
+                h0 = 4 * (c % 4)
+                nc.sync.dma_start(
+                    out=outs[c // 4][0, h0:h0 + 4].rearrange("h (m a) d -> m h (a d)", a=4),
+                    in_=r[:].rearrange("p h a d -> p h (a d)"),
+                )
+
+        def out_tile(c, a):
+            wc, ws = codes[c]
+            ps = psm.tile([P, 512], F32, name="ps", tag="ps")
+            for g in range(4):
+                nc.tensor.matmul_mx(out=ps[:], lhsT=xq[:, g, a, :].bitcast(E5X4), lhsT_scale=xsc[:, g, a, :],
+                                    rhs=wc[:, g, :].bitcast(E5X4), rhs_scale=ws[:, g, :],
+                                    start=(g == 0), stop=(g == 3))
+            if a == 0:
+                rout[c] = rp.tile([P, 4, 4, 128], F32, name="r", tag="r")
+            pa = abp.tile([P, 512], F32, name="pa", tag="pa")
+            pb = abp.tile([P, 512], F32, name="pb", tag="pb")
+            psv = ps[:].rearrange("p (h d) -> p h d", h=4)
+            nc.vector.tensor_tensor(out=pa[:].rearrange("p (h d) -> p h d", h=4), in0=psv,
+                                    in1=cosT[:, a].rearrange("p i e -> p (i e)").unsqueeze(1).to_broadcast([P, 4, 128]),
+                                    op=ALU.mult)
+            nc.vector.tensor_tensor(out=pb[:].rearrange("p (h d) -> p h d", h=4), in0=psv,
+                                    in1=sinT[:, a].rearrange("p i e -> p (i e)").unsqueeze(1).to_broadcast([P, 4, 128]),
+                                    op=ALU.mult)
+            while pend:
+                finish(*pend.pop(0))
+            pend.append((c, a, pa, pb))
+
+        done = 0
+        for s in range(len(units) + 1):
+            if s < len(units):
+                interleave(s)
+            if s >= 1:
+                quantise(s - 1)
+            target = int(RATE * (s - 8))
+            while done < min(target, len(tiles)) and last_unit[tiles[done][0]] <= s - 1:
+                out_tile(*tiles[done])
+                done += 1
+        while done < len(tiles):
+            out_tile(*tiles[done])
+            done += 1
+        while pend:
+            finish(*pend.pop(0))

@@ -16,9 +16,11 @@ ACT = mybir.ActivationFunctionType
 P = 128
 FLOPS = 2 * 512 * 2048 * 4096
 
-V_UNITS = (1, 3, 5)
-RAW_BUFS = 10
-RATE = 1.15
+V_UNITS = (1, 2, 3, 5, 9, 14, 19, 24)
+LEAD = 4
+A0 = 2
+MXLEAD = 3
+MANUAL = True
 
 
 def tile_multiheadselfattention_pa_kernel(tc, x, Wq, Wk, out_0, out_1):
@@ -27,39 +29,59 @@ def tile_multiheadselfattention_pa_kernel(tc, x, Wq, Wk, out_0, out_1):
     outs = (out_0, out_1)
 
     with ExitStack() as ctx:
+        if MANUAL:
+            ctx.enter_context(tc.manual_schedule())
         cst = ctx.enter_context(tc.tile_pool(name="cst", bufs=1))
-        rawp = ctx.enter_context(tc.tile_pool(name="rawp", bufs=RAW_BUFS))
+        rawh = ctx.enter_context(tc.tile_pool(name="rawh", bufs=8))
+        rawp = ctx.enter_context(tc.tile_pool(name="rawp", bufs=6))
         xrp = ctx.enter_context(tc.tile_pool(name="xrp", bufs=4))
         gxp = ctx.enter_context(tc.tile_pool(name="gxp", bufs=2))
-        gwp = ctx.enter_context(tc.tile_pool(name="gwp", bufs=6))
+        gws = ctx.enter_context(tc.tile_pool(name="gws", bufs=4))
+        gwv = ctx.enter_context(tc.tile_pool(name="gwv", bufs=2))
         cdp = ctx.enter_context(tc.tile_pool(name="cdp", bufs=3))
-        abp = ctx.enter_context(tc.tile_pool(name="abp", bufs=3))
+        abp = ctx.enter_context(tc.tile_pool(name="abp", bufs=4))
         rp = ctx.enter_context(tc.tile_pool(name="rp", bufs=3))
         psx = ctx.enter_context(tc.psum_pool(name="psx", bufs=2))
         psm = ctx.enter_context(tc.psum_pool(name="psm", bufs=6))
 
+        units = [(c, g) for c in range(8) for g in range(4)]
+
         raw = {}
         xraw = {}
+        big_users = {}
 
-        def load_w(mat, hf, g):
+        def load_unit(s):
+            c, g = units[s]
+            t = rawh.tile([P, 4, 512], BF16, name="wrawh", tag="wrawh")
+            nc.sync.dma_start(
+                out=t[:],
+                in_=mats[c // 4][512 * g:512 * (g + 1), 512 * (c % 4):512 * (c % 4 + 1)].rearrange("(p j) w -> p j w", j=4),
+            )
+            raw[s] = (t, 0)
+
+        def load_pair(pr, g):
+            mat, hf = pr // 2, pr % 2
             t = rawp.tile([P, 4, 1024], BF16, name="wraw", tag="wraw")
             nc.sync.dma_start(
                 out=t[:],
                 in_=mats[mat][512 * g:512 * (g + 1), 1024 * hf:1024 * (hf + 1)].rearrange("(p j) w -> p j w", j=4),
             )
-            raw[(mat, hf, g)] = t
+            raw[8 * pr + g] = (t, 0)
+            raw[8 * pr + 4 + g] = (t, 512)
 
         def load_x(g):
             t = xrp.tile([P, 4, 512], BF16, name="xraw", tag="xraw")
             nc.sync.dma_start(out=t[:], in_=x[0, :, 512 * g:512 * (g + 1)].rearrange("(m a) k -> m a k", a=4))
             xraw[g] = t
 
-        for g in range(4):
-            load_w(0, 0, g)
-            load_x(g)
-        for mat, hf in ((0, 1), (1, 0), (1, 1)):
+        for s in range(4):
+            load_unit(s)
+            load_x(s)
+        for s in range(4, 8):
+            load_unit(s)
+        for pr in range(1, 4):
             for g in range(4):
-                load_w(mat, hf, g)
+                load_pair(pr, g)
 
         ident = cst.tile([P, P], F32, name="ident")
         make_identity(nc, ident[:])
@@ -67,6 +89,8 @@ def tile_multiheadselfattention_pa_kernel(tc, x, Wq, Wk, out_0, out_1):
         nc.gpsimd.iota(pos[:], pattern=[[1, 4]], base=0, channel_multiplier=4, allow_small_or_imprecise_dtypes=True)
         ones = cst.tile([P, 8], F32, name="ones")
         nc.vector.memset(ones[:], 1.0)
+        warm = cst.tile([P, 8], F32, name="warm")
+        nc.scalar.activation(out=warm[:], in_=ones[:], func=ACT.Sin, scale=1.0)
         t0 = cst.tile([P, 8, 8], F32, name="t0")
         t1 = cst.tile([P, 8, 8], F32, name="t1")
         for k in range(8):
@@ -91,14 +115,18 @@ def tile_multiheadselfattention_pa_kernel(tc, x, Wq, Wk, out_0, out_1):
                                        op1=ALU.subtract)
         cosT = cst.tile([P, 4, 64, 2], F32, name="cosT")
         sinT = cst.tile([P, 4, 64, 2], F32, name="sinT")
-        nc.scalar.activation(out=cosT[:], in_=nfrac[:, 1].unsqueeze(3).to_broadcast([P, 4, 64, 2]), func=ACT.Sin,
-                             scale=-2.0 * math.pi)
-        nc.scalar.activation(out=sinT[:, :, :, 0], in_=nfrac[:, 0], func=ACT.Sin, scale=-2.0 * math.pi)
-        nc.scalar.activation(out=sinT[:, :, :, 1], in_=nfrac[:, 0], func=ACT.Sin, scale=2.0 * math.pi)
+
+        def sin_tables():
+            nc.scalar.activation(out=cosT[:], in_=nfrac[:, 1].unsqueeze(3).to_broadcast([P, 4, 64, 2]), func=ACT.Sin,
+                                 scale=-2.0 * math.pi)
+            nc.scalar.activation(out=sinT[:, :, :, 0], in_=nfrac[:, 0], func=ACT.Sin, scale=-2.0 * math.pi)
+            nc.scalar.activation(out=sinT[:, :, :, 1], in_=nfrac[:, 0], func=ACT.Sin, scale=2.0 * math.pi)
 
         xq = cst.tile([P, 4, 4, 128], U32, name="xq", align_bytes=64)
         xsc = cst.tile([P, 4, 4, 128], U8, name="xsc", align_bytes=64)
-        for g in range(4):
+        gxs = {}
+
+        def x_turn(g):
             xw = xraw[g][:].rearrange("p a k -> p (a k)").bitcast(F32)
             gx = gxp.tile([P, 4, 128, 2], F32, name="gx", tag="gx", align_bytes=64)
             for h2 in range(2):
@@ -109,36 +137,27 @@ def tile_multiheadselfattention_pa_kernel(tc, x, Wq, Wk, out_0, out_1):
                         nc.tensor.transpose(out=xt[:, a2, u, :], in_=xw[:, 256 * a + u:256 * (a + 1):2],
                                             identity=ident[:])
                 nc.scalar.copy(out=gx[:, 2 * h2:2 * h2 + 2], in_=xt[:].rearrange("p a u m -> p a m u"))
+            gxs[g] = gx
+
+        def x_quantise(g):
             nc.vector.quantize_mx(
                 out=xq[:, g].rearrange("p a m -> p (a m)").bitcast(E5X4),
                 scales=xsc[:, g].rearrange("p a m -> p (a m)"),
-                in_=gx[:].rearrange("p a m u -> p (a m u)").bitcast(BF16),
+                in_=gxs[g][:].rearrange("p a m u -> p (a m u)").bitcast(BF16),
             )
-
-        units = []
-        for g in range(4):
-            units.extend([(0, g), (1, g)])
-        for c in range(2, 8):
-            units.extend([(c, g) for g in range(4)])
-        last_unit = {}
-        for s, (c, g) in enumerate(units):
-            last_unit[c] = s
-        tiles = [(c, a) for c in range(8) for a in range(4)]
 
         codes = {}
         grouped = {}
         rout = {}
-        pend = []
 
         def interleave(s):
-            c, g = units[s]
-            src = raw[(c // 4, (c % 4) // 2, g)]
-            w0 = 512 * (c % 2)
-            gw = gwp.tile([P, 512, 4], BF16, name="gw", tag="gw", align_bytes=64)
+            src, w0 = raw[s]
             view = src[:, :, w0:w0 + 512].rearrange("p j w -> p w j")
             if s in V_UNITS:
+                gw = gwv.tile([P, 512, 4], BF16, name="gwv", tag="gwv", align_bytes=64)
                 nc.vector.tensor_copy(out=gw[:], in_=view)
             else:
+                gw = gws.tile([P, 512, 4], BF16, name="gws", tag="gws", align_bytes=64)
                 nc.scalar.copy(out=gw[:], in_=view)
             grouped[s] = gw
 
@@ -152,55 +171,98 @@ def tile_multiheadselfattention_pa_kernel(tc, x, Wq, Wk, out_0, out_1):
             nc.vector.quantize_mx(out=wc[:, g, :].bitcast(E5X4), scales=ws[:, g, :],
                                   in_=grouped[s][:].rearrange("p w j -> p (w j)"))
 
-        def finish(c, a, pa, pb):
-            r = rout[c]
-            nc.vector.tensor_tensor(
-                out=r[:, :, a, :].rearrange("p h (i e) -> p h i e", e=2),
-                in0=pa[:].rearrange("p (h i e) -> p h i e", h=4, e=2),
-                in1=pb[:].rearrange("p (h i e) -> p h i e", h=4, e=2)[:, :, :, ::-1],
-                op=ALU.add,
-            )
-            if a == 3:
-                h0 = 4 * (c % 4)
-                nc.sync.dma_start(
-                    out=outs[c // 4][0, h0:h0 + 4].rearrange("h (m a) d -> m h (a d)", a=4),
-                    in_=r[:].rearrange("p h a d -> p h (a d)"),
-                )
+        acc = {}
+        prod = {}
 
-        def out_tile(c, a):
+        def matmuls(t):
+            c, a = t // 4, t % 4
             wc, ws = codes[c]
             ps = psm.tile([P, 512], F32, name="ps", tag="ps")
             for g in range(4):
                 nc.tensor.matmul_mx(out=ps[:], lhsT=xq[:, g, a, :].bitcast(E5X4), lhsT_scale=xsc[:, g, a, :],
                                     rhs=wc[:, g, :].bitcast(E5X4), rhs_scale=ws[:, g, :],
                                     start=(g == 0), stop=(g == 3))
-            if a == 0:
-                rout[c] = rp.tile([P, 4, 4, 128], F32, name="r", tag="r")
+            acc[t] = ps
+
+        def products(t):
+            a = t % 4
             pa = abp.tile([P, 512], F32, name="pa", tag="pa")
             pb = abp.tile([P, 512], F32, name="pb", tag="pb")
-            psv = ps[:].rearrange("p (h d) -> p h d", h=4)
+            psv = acc[t][:].rearrange("p (h d) -> p h d", h=4)
             nc.vector.tensor_tensor(out=pa[:].rearrange("p (h d) -> p h d", h=4), in0=psv,
                                     in1=cosT[:, a].rearrange("p i e -> p (i e)").unsqueeze(1).to_broadcast([P, 4, 128]),
                                     op=ALU.mult)
             nc.vector.tensor_tensor(out=pb[:].rearrange("p (h d) -> p h d", h=4), in0=psv,
                                     in1=sinT[:, a].rearrange("p i e -> p (i e)").unsqueeze(1).to_broadcast([P, 4, 128]),
                                     op=ALU.mult)
-            while pend:
-                finish(*pend.pop(0))
-            pend.append((c, a, pa, pb))
+            prod[t] = (pa, pb)
 
-        done = 0
-        for s in range(len(units) + 1):
-            if s < len(units):
+        def finish(t):
+            c, a = t // 4, t % 4
+            if a == 0:
+                rout[c] = rp.tile([P, 4, 4, 128], F32, name="r", tag="r")
+            r = rout[c]
+            pa, pb = prod[t]
+            nc.gpsimd.tensor_tensor(
+                out=r[:, :, a, :].rearrange("p h (i e) -> p h i e", e=2),
+                in0=pa[:].rearrange("p (h i e) -> p h i e", h=4, e=2),
+                in1=pb[:].rearrange("p (h i e) -> p h i e", h=4, e=2)[:, :, :, ::-1],
+                op=ALU.add,
+            )
+            h0 = 4 * (c % 4)
+            dst = outs[c // 4][0, h0:h0 + 4].rearrange("h (m a) d -> m h a d", a=4)
+            if c == 7:
+                nc.sync.dma_start(out=dst[:, :, a, :], in_=r[:, :, a, :])
+            elif a == 3:
+                nc.sync.dma_start(out=dst.rearrange("m h a d -> m h (a d)"), in_=r[:].rearrange("p h a d -> p h (a d)"))
+
+        work = []
+        for s in range(32):
+            if s in V_UNITS:
+                work.append(("I", s))
+            work.append(("Q", s))
+            if s < 4:
+                work.append(("X", s))
+        state = {"s": 0, "w": 0, "q": 0, "x": 0, "m": 0}
+
+        def scalar_ahead(upto):
+            while state["s"] <= min(upto, 31):
+                s = state["s"]
+                if s not in V_UNITS:
+                    interleave(s)
+                if s == 0:
+                    sin_tables()
+                if s < 4:
+                    x_turn(s)
+                state["s"] = s + 1
+
+        def vector_next():
+            kind, s = work[state["w"]]
+            state["w"] += 1
+            if kind == "I":
                 interleave(s)
-            if s >= 1:
-                quantise(s - 1)
-            target = int(RATE * (s - 8))
-            while done < min(target, len(tiles)) and last_unit[tiles[done][0]] <= s - 1:
-                out_tile(*tiles[done])
-                done += 1
-        while done < len(tiles):
-            out_tile(*tiles[done])
-            done += 1
-        while pend:
-            finish(*pend.pop(0))
+            elif kind == "X":
+                x_quantise(s)
+                state["x"] += 1
+            else:
+                quantise(s)
+                state["q"] = s + 1
+                scalar_ahead(s + 1 + LEAD)
+
+        def tensor_ahead(upto):
+            while state["m"] <= min(upto, 31) and 4 * (state["m"] // 4) + 3 < state["q"] and state["x"] >= 4:
+                matmuls(state["m"])
+                state["m"] += 1
+
+        scalar_ahead(LEAD)
+        while state["q"] < 4 + A0:
+            vector_next()
+        for t in range(32):
+            tensor_ahead(t + MXLEAD)
+            products(t)
+            while state["w"] < len(work) and state["q"] < t + 5 + A0:
+                vector_next()
+            tensor_ahead(t + MXLEAD)
+            if t >= 1:
+                finish(t - 1)
+        finish(31)

@@ -119,8 +119,8 @@ def tile_multiheadselfattention_pa_kernel(tc, x, Wq, Wk, out_0, out_1):
         def sin_tables():
             nc.scalar.activation(out=cosT[:], in_=nfrac[:, 1].unsqueeze(3).to_broadcast([P, 4, 64, 2]), func=ACT.Sin,
                                  scale=-2.0 * math.pi)
-            nc.scalar.activation(out=sinT[:, :, :, 0], in_=nfrac[:, 0], func=ACT.Sin, scale=-2.0 * math.pi)
-            nc.scalar.activation(out=sinT[:, :, :, 1], in_=nfrac[:, 0], func=ACT.Sin, scale=2.0 * math.pi)
+            nc.scalar.activation(out=sinT[:, :, :, 0], in_=nfrac[:, 0], func=ACT.Sin, scale=2.0 * math.pi)
+            nc.scalar.activation(out=sinT[:, :, :, 1], in_=nfrac[:, 0], func=ACT.Sin, scale=-2.0 * math.pi)
 
         xq = cst.tile([P, 4, 4, 128], U32, name="xq", align_bytes=64)
         xsc = cst.tile([P, 4, 4, 128], U8, name="xsc", align_bytes=64)
@@ -192,8 +192,9 @@ def tile_multiheadselfattention_pa_kernel(tc, x, Wq, Wk, out_0, out_1):
             nc.vector.tensor_tensor(out=pa[:].rearrange("p (h d) -> p h d", h=4), in0=psv,
                                     in1=cosT[:, a].rearrange("p i e -> p (i e)").unsqueeze(1).to_broadcast([P, 4, 128]),
                                     op=ALU.mult)
-            nc.vector.tensor_tensor(out=pb[:].rearrange("p (h d) -> p h d", h=4), in0=psv,
-                                    in1=sinT[:, a].rearrange("p i e -> p (i e)").unsqueeze(1).to_broadcast([P, 4, 128]),
+            nc.vector.tensor_tensor(out=pb[:].rearrange("p (h i e) -> p h i e", h=4, e=2),
+                                    in0=acc[t][:].rearrange("p (h i e) -> p h i e", h=4, e=2)[:, :, :, ::-1],
+                                    in1=sinT[:, a].unsqueeze(1).to_broadcast([P, 4, 64, 2]),
                                     op=ALU.mult)
             prod[t] = (pa, pb)
 
@@ -204,9 +205,9 @@ def tile_multiheadselfattention_pa_kernel(tc, x, Wq, Wk, out_0, out_1):
             r = rout[c]
             pa, pb = prod[t]
             nc.gpsimd.tensor_tensor(
-                out=r[:, :, a, :].rearrange("p h (i e) -> p h i e", e=2),
-                in0=pa[:].rearrange("p (h i e) -> p h i e", h=4, e=2),
-                in1=pb[:].rearrange("p (h i e) -> p h i e", h=4, e=2)[:, :, :, ::-1],
+                out=r[:, :, a, :],
+                in0=pa[:].rearrange("p (h d) -> p h d", h=4),
+                in1=pb[:].rearrange("p (h d) -> p h d", h=4),
                 op=ALU.add,
             )
             h0 = 4 * (c % 4)

@@ -16,11 +16,12 @@ ACT = mybir.ActivationFunctionType
 P = 128
 FLOPS = 2 * 512 * 2048 * 4096
 
-V_UNITS = (1, 2, 3, 5, 9, 14, 19, 24)
-LEAD = 4
-A0 = 2
-MXLEAD = 3
-MANUAL = True
+V_UNITS = (1, 2, 3, 5, 7, 9, 11)
+P_UNITS = (13, 17, 19, 21, 23, 27, 29, 31)
+LEAD = 3
+Q0 = 3
+MXLEAD = 4
+RAWP = 6
 
 
 def tile_multiheadselfattention_pa_kernel(tc, x, Wq, Wk, out_0, out_1):
@@ -29,18 +30,15 @@ def tile_multiheadselfattention_pa_kernel(tc, x, Wq, Wk, out_0, out_1):
     outs = (out_0, out_1)
 
     with ExitStack() as ctx:
-        if MANUAL:
-            ctx.enter_context(tc.manual_schedule())
+        ctx.enter_context(tc.manual_schedule())
         cst = ctx.enter_context(tc.tile_pool(name="cst", bufs=1))
         rawh = ctx.enter_context(tc.tile_pool(name="rawh", bufs=8))
-        rawp = ctx.enter_context(tc.tile_pool(name="rawp", bufs=6))
-        xrp = ctx.enter_context(tc.tile_pool(name="xrp", bufs=4))
+        rawp = ctx.enter_context(tc.tile_pool(name="rawp", bufs=RAWP))
         gxp = ctx.enter_context(tc.tile_pool(name="gxp", bufs=2))
-        gws = ctx.enter_context(tc.tile_pool(name="gws", bufs=4))
-        gwv = ctx.enter_context(tc.tile_pool(name="gwv", bufs=2))
+        gwp = ctx.enter_context(tc.tile_pool(name="gwp", bufs=3))
         cdp = ctx.enter_context(tc.tile_pool(name="cdp", bufs=3))
-        abp = ctx.enter_context(tc.tile_pool(name="abp", bufs=4))
-        rp = ctx.enter_context(tc.tile_pool(name="rp", bufs=3))
+        abp = ctx.enter_context(tc.tile_pool(name="abp", bufs=3))
+        rp = ctx.enter_context(tc.tile_pool(name="rp", bufs=5))
         psx = ctx.enter_context(tc.psum_pool(name="psx", bufs=2))
         psm = ctx.enter_context(tc.psum_pool(name="psm", bufs=6))
 
@@ -48,7 +46,9 @@ def tile_multiheadselfattention_pa_kernel(tc, x, Wq, Wk, out_0, out_1):
 
         raw = {}
         xraw = {}
-        big_users = {}
+        pair_list = [(pr, g) for pr in range(1, 4) for g in range(4)]
+        copied = set()
+        loaded = {"n": 0}
 
         def load_unit(s):
             c, g = units[s]
@@ -59,18 +59,26 @@ def tile_multiheadselfattention_pa_kernel(tc, x, Wq, Wk, out_0, out_1):
             )
             raw[s] = (t, 0)
 
-        def load_pair(pr, g):
-            mat, hf = pr // 2, pr % 2
-            t = rawp.tile([P, 4, 1024], BF16, name="wraw", tag="wraw")
-            nc.sync.dma_start(
-                out=t[:],
-                in_=mats[mat][512 * g:512 * (g + 1), 1024 * hf:1024 * (hf + 1)].rearrange("(p j) w -> p j w", j=4),
-            )
-            raw[8 * pr + g] = (t, 0)
-            raw[8 * pr + 4 + g] = (t, 512)
+        def load_pairs():
+            while loaded["n"] < len(pair_list):
+                n = loaded["n"]
+                if n >= RAWP:
+                    opr, og = pair_list[n - RAWP]
+                    if (8 * opr + og) not in copied or (8 * opr + 4 + og) not in copied:
+                        return
+                pr, g = pair_list[n]
+                mat, hf = pr // 2, pr % 2
+                t = rawp.tile([P, 4, 1024], BF16, name="wraw", tag="wraw")
+                nc.sync.dma_start(
+                    out=t[:],
+                    in_=mats[mat][512 * g:512 * (g + 1), 1024 * hf:1024 * (hf + 1)].rearrange("(p j) w -> p j w", j=4),
+                )
+                raw[8 * pr + g] = (t, 0)
+                raw[8 * pr + 4 + g] = (t, 512)
+                loaded["n"] = n + 1
 
         def load_x(g):
-            t = xrp.tile([P, 4, 512], BF16, name="xraw", tag="xraw")
+            t = rp.tile([P, 4, 512], BF16, name="xraw", tag="r")
             nc.sync.dma_start(out=t[:], in_=x[0, :, 512 * g:512 * (g + 1)].rearrange("(m a) k -> m a k", a=4))
             xraw[g] = t
 
@@ -79,12 +87,13 @@ def tile_multiheadselfattention_pa_kernel(tc, x, Wq, Wk, out_0, out_1):
             load_x(s)
         for s in range(4, 8):
             load_unit(s)
-        for pr in range(1, 4):
-            for g in range(4):
-                load_pair(pr, g)
+        load_pairs()
 
         ident = cst.tile([P, P], F32, name="ident")
         make_identity(nc, ident[:])
+        identb = cst.tile([P, P], BF16, name="identb")
+        if P_UNITS:
+            make_identity(nc, identb[:])
         pos = cst.tile([P, 4], F32, name="pos")
         nc.gpsimd.iota(pos[:], pattern=[[1, 4]], base=0, channel_multiplier=4, allow_small_or_imprecise_dtypes=True)
         ones = cst.tile([P, 8], F32, name="ones")
@@ -149,27 +158,49 @@ def tile_multiheadselfattention_pa_kernel(tc, x, Wq, Wk, out_0, out_1):
         codes = {}
         grouped = {}
         rout = {}
+        banks = {}
+
+        def grouped_half(s):
+            du = s // 2
+            if du not in grouped:
+                grouped[du] = gwp.tile([P, 2, 512, 4], BF16, name="gw", tag="gw", align_bytes=64)
+            return grouped[du][:, s % 2]
+
+        def tensor_copy_unit(s):
+            src, w0 = raw[s]
+            banks[s] = []
+            for h in range(2):
+                pc = psx.tile([P, 256, 4], BF16, name="pc", tag="xt")
+                for q in range(2):
+                    wa = w0 + 256 * h + 128 * q
+                    nc.tensor.matmul(out=pc[:, 128 * q:128 * (q + 1), :], lhsT=identb[:],
+                                     rhs=src[:, :, wa:wa + 128].rearrange("p j w -> p w j"), start=True, stop=True)
+                banks[s].append(pc)
 
         def interleave(s):
             src, w0 = raw[s]
+            dst = grouped_half(s)
             view = src[:, :, w0:w0 + 512].rearrange("p j w -> p w j")
             if s in V_UNITS:
-                gw = gwv.tile([P, 512, 4], BF16, name="gwv", tag="gwv", align_bytes=64)
-                nc.vector.tensor_copy(out=gw[:], in_=view)
+                nc.vector.tensor_copy(out=dst, in_=view)
+            elif s in P_UNITS:
+                for h in range(2):
+                    nc.scalar.copy(out=dst[:, 256 * h:256 * (h + 1), :], in_=banks[s][h][:])
             else:
-                gw = gws.tile([P, 512, 4], BF16, name="gws", tag="gws", align_bytes=64)
-                nc.scalar.copy(out=gw[:], in_=view)
-            grouped[s] = gw
+                nc.scalar.copy(out=dst, in_=view)
+            copied.add(s)
+            load_pairs()
 
-        def quantise(s):
-            c, g = units[s]
+        def quantise(du):
+            c, gg = du // 2, du % 2
             if c not in codes:
                 wc = cdp.tile([P, 4, 512], U32, name="wc", tag="wc", align_bytes=64)
                 ws = cdp.tile([P, 4, 512], U8, name="ws", tag="ws", align_bytes=64)
                 codes[c] = (wc, ws)
             wc, ws = codes[c]
-            nc.vector.quantize_mx(out=wc[:, g, :].bitcast(E5X4), scales=ws[:, g, :],
-                                  in_=grouped[s][:].rearrange("p w j -> p (w j)"))
+            nc.vector.quantize_mx(out=wc[:, 2 * gg:2 * gg + 2, :].rearrange("p g w -> p (g w)").bitcast(E5X4),
+                                  scales=ws[:, 2 * gg:2 * gg + 2, :].rearrange("p g w -> p (g w)"),
+                                  in_=grouped[du][:].rearrange("p g w j -> p (g w j)"))
 
         acc = {}
         prod = {}
@@ -186,49 +217,58 @@ def tile_multiheadselfattention_pa_kernel(tc, x, Wq, Wk, out_0, out_1):
 
         def products(t):
             a = t % 4
-            pa = abp.tile([P, 512], F32, name="pa", tag="pa")
-            pb = abp.tile([P, 512], F32, name="pb", tag="pb")
+            tp = t // 2
+            if tp not in prod:
+                pa = abp.tile([P, 4, 2, 128], F32, name="pa", tag="pa")
+                pb = abp.tile([P, 4, 2, 128], F32, name="pb", tag="pb")
+                prod[tp] = (pa, pb)
+            pa, pb = prod[tp]
             psv = acc[t][:].rearrange("p (h d) -> p h d", h=4)
-            nc.vector.tensor_tensor(out=pa[:].rearrange("p (h d) -> p h d", h=4), in0=psv,
+            nc.vector.tensor_tensor(out=pa[:, :, t % 2, :], in0=psv,
                                     in1=cosT[:, a].rearrange("p i e -> p (i e)").unsqueeze(1).to_broadcast([P, 4, 128]),
                                     op=ALU.mult)
-            nc.vector.tensor_tensor(out=pb[:].rearrange("p (h i e) -> p h i e", h=4, e=2),
+            nc.vector.tensor_tensor(out=pb[:, :, t % 2, :].rearrange("p h (i e) -> p h i e", e=2),
                                     in0=acc[t][:].rearrange("p (h i e) -> p h i e", h=4, e=2)[:, :, :, ::-1],
                                     in1=sinT[:, a].unsqueeze(1).to_broadcast([P, 4, 64, 2]),
                                     op=ALU.mult)
-            prod[t] = (pa, pb)
 
-        def finish(t):
-            c, a = t // 4, t % 4
-            if a == 0:
+        def finish(tp):
+            c, a0 = tp // 2, 2 * (tp % 2)
+            if a0 == 0:
                 rout[c] = rp.tile([P, 4, 4, 128], F32, name="r", tag="r")
             r = rout[c]
-            pa, pb = prod[t]
-            nc.gpsimd.tensor_tensor(
-                out=r[:, :, a, :],
-                in0=pa[:].rearrange("p (h d) -> p h d", h=4),
-                in1=pb[:].rearrange("p (h d) -> p h d", h=4),
+            pa, pb = prod[tp]
+            eng = nc.vector if tp == 15 else nc.gpsimd
+            eng.tensor_tensor(
+                out=r[:, :, a0:a0 + 2, :].rearrange("p h a d -> p h (a d)"),
+                in0=pa[:].rearrange("p h a d -> p h (a d)"),
+                in1=pb[:].rearrange("p h a d -> p h (a d)"),
                 op=ALU.add,
             )
             h0 = 4 * (c % 4)
             dst = outs[c // 4][0, h0:h0 + 4].rearrange("h (m a) d -> m h a d", a=4)
             if c == 7:
-                nc.sync.dma_start(out=dst[:, :, a, :], in_=r[:, :, a, :])
-            elif a == 3:
+                nc.sync.dma_start(out=dst[:, :, a0:a0 + 2, :].rearrange("m h a d -> m h (a d)"),
+                                  in_=r[:, :, a0:a0 + 2, :].rearrange("p h a d -> p h (a d)"))
+            elif a0 == 2:
                 nc.sync.dma_start(out=dst.rearrange("m h a d -> m h (a d)"), in_=r[:].rearrange("p h a d -> p h (a d)"))
 
         work = []
-        for s in range(32):
-            if s in V_UNITS:
-                work.append(("I", s))
-            work.append(("Q", s))
-            if s < 4:
-                work.append(("X", s))
+        for du in range(16):
+            for s in (2 * du, 2 * du + 1):
+                if s in V_UNITS:
+                    work.append(("I", s))
+            work.append(("Q", du))
+            if du < 2:
+                work.append(("X", 2 * du))
+                work.append(("X", 2 * du + 1))
         state = {"s": 0, "w": 0, "q": 0, "x": 0, "m": 0}
 
         def scalar_ahead(upto):
             while state["s"] <= min(upto, 31):
                 s = state["s"]
+                if s in P_UNITS:
+                    tensor_copy_unit(s)
                 if s not in V_UNITS:
                     interleave(s)
                 if s == 0:
@@ -248,22 +288,21 @@ def tile_multiheadselfattention_pa_kernel(tc, x, Wq, Wk, out_0, out_1):
             else:
                 quantise(s)
                 state["q"] = s + 1
-                scalar_ahead(s + 1 + LEAD)
+                scalar_ahead(2 * (s + 1) + 1 + LEAD)
 
         def tensor_ahead(upto):
-            while state["m"] <= min(upto, 31) and 4 * (state["m"] // 4) + 3 < state["q"] and state["x"] >= 4:
+            while state["m"] <= min(upto, 31) and 2 * (state["m"] // 4) + 1 < state["q"] and state["x"] >= 4:
                 matmuls(state["m"])
                 state["m"] += 1
 
         scalar_ahead(LEAD)
-        while state["q"] < 4 + A0:
+        while state["q"] < Q0:
             vector_next()
-        for t in range(32):
-            tensor_ahead(t + MXLEAD)
-            products(t)
-            while state["w"] < len(work) and state["q"] < t + 5 + A0:
+        for tp in range(16):
+            tensor_ahead(2 * tp + 1 + MXLEAD)
+            products(2 * tp)
+            products(2 * tp + 1)
+            while state["w"] < len(work) and state["q"] < min(16, Q0 + tp + 1):
                 vector_next()
-            tensor_ahead(t + MXLEAD)
-            if t >= 1:
-                finish(t - 1)
-        finish(31)
+            tensor_ahead(2 * tp + 1 + MXLEAD)
+            finish(tp)

@@ -16,12 +16,11 @@ ACT = mybir.ActivationFunctionType
 P = 128
 FLOPS = 2 * 512 * 2048 * 4096
 
-V_UNITS = (1, 2, 3, 5, 7, 9, 11)
-P_UNITS = (13, 17, 19, 21, 23, 27, 29, 31)
-LEAD = 3
-Q0 = 3
-MXLEAD = 4
-RAWP = 6
+V_UNITS = (0, 2, 5, 7, 17, 27)
+LEAD = 4
+A0 = 2
+MXLEAD = 3
+MANUAL = False
 
 
 def tile_multiheadselfattention_pa_kernel(tc, x, Wq, Wk, out_0, out_1):
@@ -30,14 +29,16 @@ def tile_multiheadselfattention_pa_kernel(tc, x, Wq, Wk, out_0, out_1):
     outs = (out_0, out_1)
 
     with ExitStack() as ctx:
-        ctx.enter_context(tc.manual_schedule())
+        if MANUAL:
+            ctx.enter_context(tc.manual_schedule())
         cst = ctx.enter_context(tc.tile_pool(name="cst", bufs=1))
         rawh = ctx.enter_context(tc.tile_pool(name="rawh", bufs=8))
-        rawp = ctx.enter_context(tc.tile_pool(name="rawp", bufs=RAWP))
+        rawp = ctx.enter_context(tc.tile_pool(name="rawp", bufs=6))
         gxp = ctx.enter_context(tc.tile_pool(name="gxp", bufs=2))
-        gwp = ctx.enter_context(tc.tile_pool(name="gwp", bufs=3))
+        gws = ctx.enter_context(tc.tile_pool(name="gws", bufs=4))
+        gwv = ctx.enter_context(tc.tile_pool(name="gwv", bufs=2))
         cdp = ctx.enter_context(tc.tile_pool(name="cdp", bufs=3))
-        abp = ctx.enter_context(tc.tile_pool(name="abp", bufs=3))
+        abp = ctx.enter_context(tc.tile_pool(name="abp", bufs=4))
         rp = ctx.enter_context(tc.tile_pool(name="rp", bufs=5))
         psx = ctx.enter_context(tc.psum_pool(name="psx", bufs=2))
         psm = ctx.enter_context(tc.psum_pool(name="psm", bufs=6))
@@ -46,9 +47,7 @@ def tile_multiheadselfattention_pa_kernel(tc, x, Wq, Wk, out_0, out_1):
 
         raw = {}
         xraw = {}
-        pair_list = [(pr, g) for pr in range(1, 4) for g in range(4)]
-        copied = set()
-        loaded = {"n": 0}
+        big_users = {}
 
         def load_unit(s):
             c, g = units[s]
@@ -59,41 +58,35 @@ def tile_multiheadselfattention_pa_kernel(tc, x, Wq, Wk, out_0, out_1):
             )
             raw[s] = (t, 0)
 
-        def load_pairs():
-            while loaded["n"] < len(pair_list):
-                n = loaded["n"]
-                if n >= RAWP:
-                    opr, og = pair_list[n - RAWP]
-                    if (8 * opr + og) not in copied or (8 * opr + 4 + og) not in copied:
-                        return
-                pr, g = pair_list[n]
-                mat, hf = pr // 2, pr % 2
-                t = rawp.tile([P, 4, 1024], BF16, name="wraw", tag="wraw")
-                nc.sync.dma_start(
-                    out=t[:],
-                    in_=mats[mat][512 * g:512 * (g + 1), 1024 * hf:1024 * (hf + 1)].rearrange("(p j) w -> p j w", j=4),
-                )
-                raw[8 * pr + g] = (t, 0)
-                raw[8 * pr + 4 + g] = (t, 512)
-                loaded["n"] = n + 1
+        def load_pair(pr, g):
+            mat, hf = pr // 2, pr % 2
+            t = rawp.tile([P, 4, 1024], BF16, name="wraw", tag="wraw")
+            nc.sync.dma_start(
+                out=t[:],
+                in_=mats[mat][512 * g:512 * (g + 1), 1024 * hf:1024 * (hf + 1)].rearrange("(p j) w -> p j w", j=4),
+            )
+            raw[8 * pr + g] = (t, 0)
+            raw[8 * pr + 4 + g] = (t, 512)
 
-        def load_x(g):
-            t = rp.tile([P, 4, 512], BF16, name="xraw", tag="r")
-            nc.sync.dma_start(out=t[:], in_=x[0, :, 512 * g:512 * (g + 1)].rearrange("(m a) k -> m a k", a=4))
-            xraw[g] = t
+        def load_x(a):
+            t = rp.tile([P, 2048], BF16, name="xraw", tag="r")
+            nc.sync.dma_start(out=t[:], in_=x[0].rearrange("(m a) k -> m a k", a=4)[:, a, :])
+            xraw[a] = t
 
         for s in range(4):
             load_unit(s)
-            load_x(s)
+        load_x(0)
+        load_x(1)
         for s in range(4, 8):
             load_unit(s)
-        load_pairs()
+            if s < 6:
+                load_x(s - 2)
+        for pr in range(1, 4):
+            for g in range(4):
+                load_pair(pr, g)
 
         ident = cst.tile([P, P], F32, name="ident")
         make_identity(nc, ident[:])
-        identb = cst.tile([P, P], BF16, name="identb")
-        if P_UNITS:
-            make_identity(nc, identb[:])
         pos = cst.tile([P, 4], F32, name="pos")
         nc.gpsimd.iota(pos[:], pattern=[[1, 4]], base=0, channel_multiplier=4, allow_small_or_imprecise_dtypes=True)
         ones = cst.tile([P, 8], F32, name="ones")
@@ -122,21 +115,20 @@ def tile_multiheadselfattention_pa_kernel(tc, x, Wq, Wk, out_0, out_1):
         nfrac = cst.tile([P, 2, 4, 64], F32, name="nfrac")
         nc.vector.scalar_tensor_tensor(out=nfrac[:], in0=frac[:], scalar=0.5, in1=frac[:], op0=ALU.is_ge,
                                        op1=ALU.subtract)
-        cosT = cst.tile([P, 4, 64, 2], F32, name="cosT")
-        sinT = cst.tile([P, 4, 64, 2], F32, name="sinT")
+        tabT = cst.tile([P, 4, 2, 64, 2], F32, name="tabT")
 
         def sin_tables():
-            nc.scalar.activation(out=cosT[:], in_=nfrac[:, 1].unsqueeze(3).to_broadcast([P, 4, 64, 2]), func=ACT.Sin,
+            nc.scalar.activation(out=tabT[:, :, 0], in_=nfrac[:, 1].unsqueeze(3).to_broadcast([P, 4, 64, 2]), func=ACT.Sin,
                                  scale=-2.0 * math.pi)
-            nc.scalar.activation(out=sinT[:, :, :, 0], in_=nfrac[:, 0], func=ACT.Sin, scale=2.0 * math.pi)
-            nc.scalar.activation(out=sinT[:, :, :, 1], in_=nfrac[:, 0], func=ACT.Sin, scale=-2.0 * math.pi)
+            nc.scalar.activation(out=tabT[:, :, 1, :, 0], in_=nfrac[:, 0], func=ACT.Sin, scale=-2.0 * math.pi)
+            nc.scalar.activation(out=tabT[:, :, 1, :, 1], in_=nfrac[:, 0], func=ACT.Sin, scale=2.0 * math.pi)
 
         xq = cst.tile([P, 4, 4, 128], U32, name="xq", align_bytes=64)
         xsc = cst.tile([P, 4, 4, 128], U8, name="xsc", align_bytes=64)
         gxs = {}
 
         def x_turn(g):
-            xw = xraw[g][:].rearrange("p a k -> p (a k)").bitcast(F32)
+            xw = xraw[g][:].bitcast(F32)
             gx = gxp.tile([P, 4, 128, 2], F32, name="gx", tag="gx", align_bytes=64)
             for h2 in range(2):
                 xt = psx.tile([P, 2, 2, 128], F32, name="xt", tag="xt")
@@ -145,7 +137,7 @@ def tile_multiheadselfattention_pa_kernel(tc, x, Wq, Wk, out_0, out_1):
                     for u in range(2):
                         nc.tensor.transpose(out=xt[:, a2, u, :], in_=xw[:, 256 * a + u:256 * (a + 1):2],
                                             identity=ident[:])
-                nc.scalar.copy(out=gx[:, 2 * h2:2 * h2 + 2], in_=xt[:].rearrange("p a u m -> p a m u"))
+                nc.vector.tensor_copy(out=gx[:, 2 * h2:2 * h2 + 2], in_=xt[:].rearrange("p a u m -> p a m u"))
             gxs[g] = gx
 
         def x_quantise(g):
@@ -158,49 +150,27 @@ def tile_multiheadselfattention_pa_kernel(tc, x, Wq, Wk, out_0, out_1):
         codes = {}
         grouped = {}
         rout = {}
-        banks = {}
-
-        def grouped_half(s):
-            du = s // 2
-            if du not in grouped:
-                grouped[du] = gwp.tile([P, 2, 512, 4], BF16, name="gw", tag="gw", align_bytes=64)
-            return grouped[du][:, s % 2]
-
-        def tensor_copy_unit(s):
-            src, w0 = raw[s]
-            banks[s] = []
-            for h in range(2):
-                pc = psx.tile([P, 256, 4], BF16, name="pc", tag="xt")
-                for q in range(2):
-                    wa = w0 + 256 * h + 128 * q
-                    nc.tensor.matmul(out=pc[:, 128 * q:128 * (q + 1), :], lhsT=identb[:],
-                                     rhs=src[:, :, wa:wa + 128].rearrange("p j w -> p w j"), start=True, stop=True)
-                banks[s].append(pc)
 
         def interleave(s):
             src, w0 = raw[s]
-            dst = grouped_half(s)
             view = src[:, :, w0:w0 + 512].rearrange("p j w -> p w j")
             if s in V_UNITS:
-                nc.vector.tensor_copy(out=dst, in_=view)
-            elif s in P_UNITS:
-                for h in range(2):
-                    nc.scalar.copy(out=dst[:, 256 * h:256 * (h + 1), :], in_=banks[s][h][:])
+                gw = gwv.tile([P, 512, 4], BF16, name="gwv", tag="gwv", align_bytes=64)
+                nc.vector.tensor_copy(out=gw[:], in_=view)
             else:
-                nc.scalar.copy(out=dst, in_=view)
-            copied.add(s)
-            load_pairs()
+                gw = gws.tile([P, 512, 4], BF16, name="gws", tag="gws", align_bytes=64)
+                nc.scalar.copy(out=gw[:], in_=view)
+            grouped[s] = gw
 
-        def quantise(du):
-            c, gg = du // 2, du % 2
+        def quantise(s):
+            c, g = units[s]
             if c not in codes:
                 wc = cdp.tile([P, 4, 512], U32, name="wc", tag="wc", align_bytes=64)
                 ws = cdp.tile([P, 4, 512], U8, name="ws", tag="ws", align_bytes=64)
                 codes[c] = (wc, ws)
             wc, ws = codes[c]
-            nc.vector.quantize_mx(out=wc[:, 2 * gg:2 * gg + 2, :].rearrange("p g w -> p (g w)").bitcast(E5X4),
-                                  scales=ws[:, 2 * gg:2 * gg + 2, :].rearrange("p g w -> p (g w)"),
-                                  in_=grouped[du][:].rearrange("p g w j -> p (g w j)"))
+            nc.vector.quantize_mx(out=wc[:, g, :].bitcast(E5X4), scales=ws[:, g, :],
+                                  in_=grouped[s][:].rearrange("p w j -> p (w j)"))
 
         acc = {}
         prod = {}
@@ -210,65 +180,52 @@ def tile_multiheadselfattention_pa_kernel(tc, x, Wq, Wk, out_0, out_1):
             wc, ws = codes[c]
             ps = psm.tile([P, 512], F32, name="ps", tag="ps")
             for g in range(4):
-                nc.tensor.matmul_mx(out=ps[:], lhsT=xq[:, g, a, :].bitcast(E5X4), lhsT_scale=xsc[:, g, a, :],
+                nc.tensor.matmul_mx(out=ps[:], lhsT=xq[:, a, g, :].bitcast(E5X4), lhsT_scale=xsc[:, a, g, :],
                                     rhs=wc[:, g, :].bitcast(E5X4), rhs_scale=ws[:, g, :],
                                     start=(g == 0), stop=(g == 3))
             acc[t] = ps
 
         def products(t):
             a = t % 4
-            tp = t // 2
-            if tp not in prod:
-                pa = abp.tile([P, 4, 2, 128], F32, name="pa", tag="pa")
-                pb = abp.tile([P, 4, 2, 128], F32, name="pb", tag="pb")
-                prod[tp] = (pa, pb)
-            pa, pb = prod[tp]
-            psv = acc[t][:].rearrange("p (h d) -> p h d", h=4)
-            nc.vector.tensor_tensor(out=pa[:, :, t % 2, :], in0=psv,
-                                    in1=cosT[:, a].rearrange("p i e -> p (i e)").unsqueeze(1).to_broadcast([P, 4, 128]),
+            pab = abp.tile([P, 2, 4, 128], F32, name="pab", tag="pab")
+            nc.vector.tensor_tensor(out=pab[:],
+                                    in0=acc[t][:].rearrange("p (h d) -> p h d", h=4).unsqueeze(1).to_broadcast([P, 2, 4, 128]),
+                                    in1=tabT[:, a].rearrange("p r i e -> p r (i e)").unsqueeze(2).to_broadcast([P, 2, 4, 128]),
                                     op=ALU.mult)
-            nc.vector.tensor_tensor(out=pb[:, :, t % 2, :].rearrange("p h (i e) -> p h i e", e=2),
-                                    in0=acc[t][:].rearrange("p (h i e) -> p h i e", h=4, e=2)[:, :, :, ::-1],
-                                    in1=sinT[:, a].unsqueeze(1).to_broadcast([P, 4, 64, 2]),
-                                    op=ALU.mult)
+            prod[t] = pab
 
-        def finish(tp):
-            c, a0 = tp // 2, 2 * (tp % 2)
-            if a0 == 0:
+        def finish(t):
+            c, a = t // 4, t % 4
+            if a == 0:
                 rout[c] = rp.tile([P, 4, 4, 128], F32, name="r", tag="r")
             r = rout[c]
-            pa, pb = prod[tp]
-            eng = nc.vector if tp == 15 else nc.gpsimd
+            pab = prod[t]
+            eng = nc.vector if t == 31 else nc.gpsimd
             eng.tensor_tensor(
-                out=r[:, :, a0:a0 + 2, :].rearrange("p h a d -> p h (a d)"),
-                in0=pa[:].rearrange("p h a d -> p h (a d)"),
-                in1=pb[:].rearrange("p h a d -> p h (a d)"),
+                out=r[:, :, a, :].rearrange("p h (i e) -> p h i e", e=2),
+                in0=pab[:, 0].rearrange("p h (i e) -> p h i e", e=2),
+                in1=pab[:, 1].rearrange("p h (i e) -> p h i e", e=2)[:, :, :, ::-1],
                 op=ALU.add,
             )
             h0 = 4 * (c % 4)
             dst = outs[c // 4][0, h0:h0 + 4].rearrange("h (m a) d -> m h a d", a=4)
             if c == 7:
-                nc.sync.dma_start(out=dst[:, :, a0:a0 + 2, :].rearrange("m h a d -> m h (a d)"),
-                                  in_=r[:, :, a0:a0 + 2, :].rearrange("p h a d -> p h (a d)"))
-            elif a0 == 2:
+                nc.sync.dma_start(out=dst[:, :, a, :], in_=r[:, :, a, :])
+            elif a == 3:
                 nc.sync.dma_start(out=dst.rearrange("m h a d -> m h (a d)"), in_=r[:].rearrange("p h a d -> p h (a d)"))
 
         work = []
-        for du in range(16):
-            for s in (2 * du, 2 * du + 1):
-                if s in V_UNITS:
-                    work.append(("I", s))
-            work.append(("Q", du))
-            if du < 2:
-                work.append(("X", 2 * du))
-                work.append(("X", 2 * du + 1))
+        for s in range(32):
+            if s in V_UNITS:
+                work.append(("I", s))
+            work.append(("Q", s))
+            if s < 4:
+                work.append(("X", s))
         state = {"s": 0, "w": 0, "q": 0, "x": 0, "m": 0}
 
         def scalar_ahead(upto):
             while state["s"] <= min(upto, 31):
                 s = state["s"]
-                if s in P_UNITS:
-                    tensor_copy_unit(s)
                 if s not in V_UNITS:
                     interleave(s)
                 if s == 0:
@@ -288,21 +245,22 @@ def tile_multiheadselfattention_pa_kernel(tc, x, Wq, Wk, out_0, out_1):
             else:
                 quantise(s)
                 state["q"] = s + 1
-                scalar_ahead(2 * (s + 1) + 1 + LEAD)
+                scalar_ahead(s + 1 + LEAD)
 
         def tensor_ahead(upto):
-            while state["m"] <= min(upto, 31) and 2 * (state["m"] // 4) + 1 < state["q"] and state["x"] >= 4:
+            while state["m"] <= min(upto, 31) and 4 * (state["m"] // 4) + 3 < state["q"] and state["x"] > state["m"] % 4:
                 matmuls(state["m"])
                 state["m"] += 1
 
         scalar_ahead(LEAD)
-        while state["q"] < Q0:
+        while state["q"] < 4 + A0:
             vector_next()
-        for tp in range(16):
-            tensor_ahead(2 * tp + 1 + MXLEAD)
-            products(2 * tp)
-            products(2 * tp + 1)
-            while state["w"] < len(work) and state["q"] < min(16, Q0 + tp + 1):
+        for t in range(32):
+            tensor_ahead(t + MXLEAD)
+            products(t)
+            while state["w"] < len(work) and state["q"] < t + 5 + A0:
                 vector_next()
-            tensor_ahead(2 * tp + 1 + MXLEAD)
-            finish(tp)
+            tensor_ahead(t + MXLEAD)
+            if t >= 1:
+                finish(t - 1)
+        finish(31)

@@ -153,13 +153,13 @@ def tile_multiheadselfattention_pa_kernel(tc, x, Wq, Wk, out_0, out_1):
 
         def interleave(s):
             src, w0 = raw[s]
-            view = src[:, :, w0:w0 + 512].rearrange("p j w -> p w j")
+            view = src[:, :, w0:w0 + 512].rearrange("p j (c i) -> p c j i", i=4)
             if s in V_UNITS:
                 gw = gwv.tile([P, 512, 4], BF16, name="gwv", tag="gwv", align_bytes=64)
-                nc.vector.tensor_copy(out=gw[:], in_=view)
+                nc.vector.tensor_copy(out=gw[:].rearrange("p (c i) j -> p c j i", i=4), in_=view)
             else:
                 gw = gws.tile([P, 512, 4], BF16, name="gws", tag="gws", align_bytes=64)
-                nc.scalar.copy(out=gw[:], in_=view)
+                nc.scalar.copy(out=gw[:].rearrange("p (c i) j -> p c j i", i=4), in_=view)
             grouped[s] = gw
 
         def quantise(s):

@@ -16,7 +16,8 @@ ACT = mybir.ActivationFunctionType
 P = 128
 FLOPS = 2 * 512 * 2048 * 4096
 
-V_UNITS = (0, 2, 5, 7, 17, 27)
+V_UNITS = (0, 2)
+T_UNITS = (1, 3, 6, 9, 12, 15, 18, 20, 23, 26, 28, 30)
 LEAD = 4
 A0 = 2
 MXLEAD = 3
@@ -87,6 +88,8 @@ def tile_multiheadselfattention_pa_kernel(tc, x, Wq, Wk, out_0, out_1):
 
         ident = cst.tile([P, P], F32, name="ident")
         make_identity(nc, ident[:])
+        identb = cst.tile([P, P], BF16, name="identb")
+        make_identity(nc, identb[:])
         pos = cst.tile([P, 4], F32, name="pos")
         nc.gpsimd.iota(pos[:], pattern=[[1, 4]], base=0, channel_multiplier=4, allow_small_or_imprecise_dtypes=True)
         ones = cst.tile([P, 8], F32, name="ones")
@@ -153,6 +156,18 @@ def tile_multiheadselfattention_pa_kernel(tc, x, Wq, Wk, out_0, out_1):
 
         def interleave(s):
             src, w0 = raw[s]
+            if s in T_UNITS:
+                gw = gws.tile([P, 512, 4], BF16, name="gws", tag="gws", align_bytes=64)
+                flat = gw[:].rearrange("p w j -> p (w j)")
+                for h in range(2):
+                    pi = psx.tile([P, 1024], BF16, name="pi", tag="xt")
+                    for q in range(2):
+                        c0 = w0 + 256 * h + 128 * q
+                        nc.tensor.matmul(out=pi[:, 512 * q:512 * (q + 1)], lhsT=identb[:],
+                                         rhs=src[:, :, c0:c0 + 128].rearrange("p j w -> p w j"), start=True, stop=True)
+                    nc.scalar.copy(out=flat[:, 1024 * h:1024 * (h + 1)].bitcast(F32), in_=pi[:].bitcast(F32))
+                grouped[s] = gw
+                return
             view = src[:, :, w0:w0 + 512].rearrange("p j (c i) -> p c j i", i=4)
             if s in V_UNITS:
                 gw = gwv.tile([P, 512, 4], BF16, name="gwv", tag="gwv", align_bytes=64)

@@ -160,12 +160,13 @@ def tile_multiheadselfattention_pa_kernel(tc, x, Wq, Wk, out_0, out_1):
                 gw = gws.tile([P, 512, 4], BF16, name="gws", tag="gws", align_bytes=64)
                 flat = gw[:].rearrange("p w j -> p (w j)")
                 for h in range(2):
-                    pi = psx.tile([P, 1024], BF16, name="pi", tag="xt")
-                    for q in range(2):
-                        c0 = w0 + 256 * h + 128 * q
-                        nc.tensor.matmul(out=pi[:, 512 * q:512 * (q + 1)], lhsT=identb[:],
-                                         rhs=src[:, :, c0:c0 + 128].rearrange("p j w -> p w j"), start=True, stop=True)
-                    nc.scalar.copy(out=flat[:, 1024 * h:1024 * (h + 1)].bitcast(F32), in_=pi[:].bitcast(F32))
+                    pi = psx.tile([P, 256, 4], BF16, name="pi", tag="xt")
+                    c0 = w0 + 256 * h
+                    for u in range(2):
+                        nc.tensor.matmul(out=pi[:, :, 2 * u:2 * u + 2].rearrange("p w e -> p e w"), lhsT=identb[:],
+                                         rhs=src[:, 2 * u:2 * u + 2, c0:c0 + 256], start=True, stop=True)
+                    nc.scalar.copy(out=flat[:, 1024 * h:1024 * (h + 1)].bitcast(F32),
+                                   in_=pi[:].rearrange("p w j -> p (w j)").bitcast(F32))
                 grouped[s] = gw
                 return
             view = src[:, :, w0:w0 + 512].rearrange("p j (c i) -> p c j i", i=4)

@@ -16,8 +16,8 @@ ACT = mybir.ActivationFunctionType
 P = 128
 FLOPS = 2 * 512 * 2048 * 4096
 
-V_UNITS = (0, 2)
-T_UNITS = (1, 3, 6, 9, 12, 15, 18, 20, 23, 26, 28, 30)
+V_UNITS = (0, 2, 5, 7)
+T_UNITS = (12, 17, 22, 27)
 LEAD = 4
 A0 = 2
 MXLEAD = 3

@@ -18,6 +18,7 @@ FLOPS = 2 * 512 * 2048 * 4096
 
 V_UNITS = (0, 2, 5, 7)
 T_UNITS = (12, 17, 22, 27)
+T_LEAD = 3
 LEAD = 4
 A0 = 2
 MXLEAD = 3
@@ -154,19 +155,27 @@ def tile_multiheadselfattention_pa_kernel(tc, x, Wq, Wk, out_0, out_1):
         grouped = {}
         rout = {}
 
+        filled = {}
+
+        def fill(s):
+            src, w0 = raw[s]
+            filled[s] = []
+            for h in range(2):
+                pi = psx.tile([P, 256, 4], BF16, name="pi", tag="xt")
+                c0 = w0 + 256 * h
+                for u in range(2):
+                    nc.tensor.matmul(out=pi[:, :, 2 * u:2 * u + 2].rearrange("p w e -> p e w"), lhsT=identb[:],
+                                     rhs=src[:, 2 * u:2 * u + 2, c0:c0 + 256], start=True, stop=True)
+                filled[s].append(pi)
+
         def interleave(s):
             src, w0 = raw[s]
             if s in T_UNITS:
                 gw = gws.tile([P, 512, 4], BF16, name="gws", tag="gws", align_bytes=64)
                 flat = gw[:].rearrange("p w j -> p (w j)")
                 for h in range(2):
-                    pi = psx.tile([P, 256, 4], BF16, name="pi", tag="xt")
-                    c0 = w0 + 256 * h
-                    for u in range(2):
-                        nc.tensor.matmul(out=pi[:, :, 2 * u:2 * u + 2].rearrange("p w e -> p e w"), lhsT=identb[:],
-                                         rhs=src[:, 2 * u:2 * u + 2, c0:c0 + 256], start=True, stop=True)
                     nc.scalar.copy(out=flat[:, 1024 * h:1024 * (h + 1)].bitcast(F32),
-                                   in_=pi[:].rearrange("p w j -> p (w j)").bitcast(F32))
+                                   in_=filled[s][h][:].rearrange("p w j -> p (w j)").bitcast(F32))
                 grouped[s] = gw
                 return
             view = src[:, :, w0:w0 + 512].rearrange("p j (c i) -> p c j i", i=4)
@@ -242,6 +251,8 @@ def tile_multiheadselfattention_pa_kernel(tc, x, Wq, Wk, out_0, out_1):
         def scalar_ahead(upto):
             while state["s"] <= min(upto, 31):
                 s = state["s"]
+                if s + T_LEAD in T_UNITS:
+                    fill(s + T_LEAD)
                 if s not in V_UNITS:
                     interleave(s)
                 if s == 0:

@@ -178,13 +178,13 @@ def tile_multiheadselfattention_pa_kernel(tc, x, Wq, Wk, out_0, out_1):
                                    in_=filled[s][h][:].rearrange("p w j -> p (w j)").bitcast(F32))
                 grouped[s] = gw
                 return
-            view = src[:, :, w0:w0 + 512].rearrange("p j (c i) -> p c j i", i=4)
+            view = src[:, :, w0:w0 + 512].rearrange("p j (c i) -> p c j i", i=8)
             if s in V_UNITS:
                 gw = gwv.tile([P, 512, 4], BF16, name="gwv", tag="gwv", align_bytes=64)
-                nc.vector.tensor_copy(out=gw[:].rearrange("p (c i) j -> p c j i", i=4), in_=view)
+                nc.vector.tensor_copy(out=gw[:].rearrange("p (c i) j -> p c j i", i=8), in_=view)
             else:
                 gw = gws.tile([P, 512, 4], BF16, name="gws", tag="gws", align_bytes=64)
-                nc.scalar.copy(out=gw[:].rearrange("p (c i) j -> p c j i", i=4), in_=view)
+                nc.scalar.copy(out=gw[:].rearrange("p (c i) j -> p c j i", i=8), in_=view)
             grouped[s] = gw
 
         def quantise(s):

@@ -225,7 +225,7 @@ def tile_multiheadselfattention_pa_kernel(tc, x, Wq, Wk, out_0, out_1):
                 rout[c] = rp.tile([P, 4, 4, 128], F32, name="r", tag="r")
             r = rout[c]
             pab = prod[t]
-            eng = nc.vector if t == 31 else nc.gpsimd
+            eng = nc.vector if (t % 6 == 5 or t == 31) else nc.gpsimd
             eng.tensor_tensor(
                 out=r[:, :, a, :].rearrange("p h (i e) -> p h i e", e=2),
                 in0=pab[:, 0].rearrange("p h (i e) -> p h i e", e=2),

from contextlib import ExitStack
import math

import concourse.mybir as mybir
from concourse.masks import make_identity

F32 = mybir.dt.float32
BF16 = mybir.dt.bfloat16
U32 = mybir.dt.uint32
U8 = mybir.dt.uint8
I32 = mybir.dt.int32
E5X4 = mybir.dt.float8_e5m2_x4
ALU = mybir.AluOpType
ACT = mybir.ActivationFunctionType

P = 128
FLOPS = 2 * 512 * 2048 * 4096

V_UNITS = (0, 2, 5, 7)
T_UNITS = (12, 17, 22, 27)
T_LEAD = 3
LEAD = 4
A0 = 2
MXLEAD = 3
MANUAL = False


def tile_multiheadselfattention_pa_kernel(tc, x, Wq, Wk, out_0, out_1):
    nc = tc.nc
    mats = (Wq, Wk)
    outs = (out_0, out_1)

    with ExitStack() as ctx:
        if MANUAL:
            ctx.enter_context(tc.manual_schedule())
        cst = ctx.enter_context(tc.tile_pool(name="cst", bufs=1))
        rawh = ctx.enter_context(tc.tile_pool(name="rawh", bufs=8))
        rawp = ctx.enter_context(tc.tile_pool(name="rawp", bufs=6))
        gxp = ctx.enter_context(tc.tile_pool(name="gxp", bufs=2))
        gws = ctx.enter_context(tc.tile_pool(name="gws", bufs=4))
        gwv = ctx.enter_context(tc.tile_pool(name="gwv", bufs=2))
        cdp = ctx.enter_context(tc.tile_pool(name="cdp", bufs=3))
        abp = ctx.enter_context(tc.tile_pool(name="abp", bufs=4))
        rp = ctx.enter_context(tc.tile_pool(name="rp", bufs=5))
        psx = ctx.enter_context(tc.psum_pool(name="psx", bufs=2))
        psm = ctx.enter_context(tc.psum_pool(name="psm", bufs=6))

        units = [(c, g) for c in range(8) for g in range(4)]

        raw = {}
        xraw = {}
        big_users = {}

        def load_unit(s):
            c, g = units[s]
            t = rawh.tile([P, 4, 512], BF16, name="wrawh", tag="wrawh")
            nc.sync.dma_start(
                out=t[:],
                in_=mats[c // 4][512 * g:512 * (g + 1), 512 * (c % 4):512 * (c % 4 + 1)].rearrange("(p j) w -> p j w", j=4),
            )
            raw[s] = (t, 0)

        def load_pair(pr, g):
            mat, hf = pr // 2, pr % 2
            t = rawp.tile([P, 4, 1024], BF16, name="wraw", tag="wraw")
            nc.sync.dma_start(
                out=t[:],
                in_=mats[mat][512 * g:512 * (g + 1), 1024 * hf:1024 * (hf + 1)].rearrange("(p j) w -> p j w", j=4),
            )
            raw[8 * pr + g] = (t, 0)
            raw[8 * pr + 4 + g] = (t, 512)

        def load_x(a):
            t = rp.tile([P, 2048], BF16, name="xraw", tag="r")
            nc.sync.dma_start(out=t[:], in_=x[0].rearrange("(m a) k -> m a k", a=4)[:, a, :])
            xraw[a] = t

        for s in range(4):
            load_unit(s)
        load_x(0)
        load_x(1)
        for s in range(4, 8):
            load_unit(s)
            if s < 6:
                load_x(s - 2)
        for pr in range(1, 4):
            for g in range(4):
                load_pair(pr, g)

        ident = cst.tile([P, P], F32, name="ident")
        make_identity(nc, ident[:])
        identb = cst.tile([P, P], BF16, name="identb")
        make_identity(nc, identb[:])
        pos = cst.tile([P, 4], F32, name="pos")
        nc.gpsimd.iota(pos[:], pattern=[[1, 4]], base=0, channel_multiplier=4, allow_small_or_imprecise_dtypes=True)
        ones = cst.tile([P, 8], F32, name="ones")
        nc.vector.memset(ones[:], 1.0)
        warm = cst.tile([P, 8], F32, name="warm")
        nc.scalar.activation(out=warm[:], in_=ones[:], func=ACT.Sin, scale=1.0)
        t0 = cst.tile([P, 8, 8], F32, name="t0")
        t1 = cst.tile([P, 8, 8], F32, name="t1")
        for k in range(8):
            nc.vector.tensor_scalar(out=t0[:, :, k], in0=ones[:], scalar1=10000.0 ** (-k / 64.0) / (2.0 * math.pi),
                                    scalar2=None, op0=ALU.mult)
            nc.vector.tensor_scalar(out=t1[:, k, :], in0=ones[:], scalar1=10000.0 ** (-8.0 * k / 64.0),
                                    scalar2=None, op0=ALU.mult)
        frq = cst.tile([P, 64], F32, name="frq")
        nc.vector.tensor_tensor(out=frq[:], in0=t0[:].rearrange("p a b -> p (a b)"),
                                in1=t1[:].rearrange("p a b -> p (a b)"), op=ALU.mult)
        turns = cst.tile([P, 2, 4, 64], F32, name="turns")
        for a in range(4):
            nc.vector.tensor_scalar(out=turns[:, 0, a, :], in0=frq[:], scalar1=pos[:, a:a + 1], scalar2=None,
                                    op0=ALU.mult)
        nc.vector.tensor_scalar(out=turns[:, 1], in0=turns[:, 0], scalar1=0.25, scalar2=None, op0=ALU.add)
        whole = cst.tile([P, 2, 4, 64], I32, name="whole")
        nc.vector.tensor_copy(out=whole[:], in_=turns[:])
        frac = cst.tile([P, 2, 4, 64], F32, name="frac")
        nc.vector.tensor_tensor(out=frac[:], in0=turns[:], in1=whole[:], op=ALU.subtract)
        nfrac = cst.tile([P, 2, 4, 64], F32, name="nfrac")
        nc.vector.scalar_tensor_tensor(out=nfrac[:], in0=frac[:], scalar=0.5, in1=frac[:], op0=ALU.is_ge,
                                       op1=ALU.subtract)
        tabT = cst.tile([P, 4, 2, 64, 2], F32, name="tabT")

        def sin_tables():
            nc.scalar.activation(out=tabT[:, :, 0], in_=nfrac[:, 1].unsqueeze(3).to_broadcast([P, 4, 64, 2]), func=ACT.Sin,
                                 scale=-2.0 * math.pi)
            nc.scalar.activation(out=tabT[:, :, 1, :, 0], in_=nfrac[:, 0], func=ACT.Sin, scale=-2.0 * math.pi)
            nc.scalar.activation(out=tabT[:, :, 1, :, 1], in_=nfrac[:, 0], func=ACT.Sin, scale=2.0 * math.pi)

        xq = cst.tile([P, 4, 4, 128], U32, name="xq", align_bytes=64)
        xsc = cst.tile([P, 4, 4, 128], U8, name="xsc", align_bytes=64)
        gxs = {}

        def x_turn(g):
            xw = xraw[g][:].bitcast(F32)
            gx = gxp.tile([P, 4, 128, 2], F32, name="gx", tag="gx", align_bytes=64)
            for h2 in range(2):
                xt = psx.tile([P, 2, 2, 128], F32, name="xt", tag="xt")
                for a2 in range(2):
                    a = 2 * h2 + a2
                    for u in range(2):
                        nc.tensor.transpose(out=xt[:, a2, u, :], in_=xw[:, 256 * a + u:256 * (a + 1):2],
                                            identity=ident[:])
                nc.vector.tensor_copy(out=gx[:, 2 * h2:2 * h2 + 2], in_=xt[:].rearrange("p a u m -> p a m u"))
            gxs[g] = gx

        def x_quantise(g):
            nc.vector.quantize_mx(
                out=xq[:, g].rearrange("p a m -> p (a m)").bitcast(E5X4),
                scales=xsc[:, g].rearrange("p a m -> p (a m)"),
                in_=gxs[g][:].rearrange("p a m u -> p (a m u)").bitcast(BF16),
            )

        codes = {}
        grouped = {}
        rout = {}

        filled = {}

        def fill(s):
            src, w0 = raw[s]
            filled[s] = []
            for h in range(2):
                pi = psx.tile([P, 256, 4], BF16, name="pi", tag="xt")
                c0 = w0 + 256 * h
                for u in range(2):
                    nc.tensor.matmul(out=pi[:, :, 2 * u:2 * u + 2].rearrange("p w e -> p e w"), lhsT=identb[:],
                                     rhs=src[:, 2 * u:2 * u + 2, c0:c0 + 256], start=True, stop=True)
                filled[s].append(pi)

        def interleave(s):
            src, w0 = raw[s]
            if s in T_UNITS:
                gw = gws.tile([P, 512, 4], BF16, name="gws", tag="gws", align_bytes=64)
                flat = gw[:].rearrange("p w j -> p (w j)")
                for h in range(2):
                    nc.scalar.copy(out=flat[:, 1024 * h:1024 * (h + 1)].bitcast(F32),
                                   in_=filled[s][h][:].rearrange("p w j -> p (w j)").bitcast(F32))
                grouped[s] = gw
                return
            view = src[:, :, w0:w0 + 512].rearrange("p j (c i) -> p c j i", i=8)
            if s in V_UNITS:
                gw = gwv.tile([P, 512, 4], BF16, name="gwv", tag="gwv", align_bytes=64)
                nc.vector.tensor_copy(out=gw[:].rearrange("p (c i) j -> p c j i", i=8), in_=view)
            else:
                gw = gws.tile([P, 512, 4], BF16, name="gws", tag="gws", align_bytes=64)
                nc.scalar.copy(out=gw[:].rearrange("p (c i) j -> p c j i", i=8), in_=view)
            grouped[s] = gw

        def quantise(s):
            c, g = units[s]
            if c not in codes:
                wc = cdp.tile([P, 4, 512], U32, name="wc", tag="wc", align_bytes=64)
                ws = cdp.tile([P, 4, 512], U8, name="ws", tag="ws", align_bytes=64)
                codes[c] = (wc, ws)
            wc, ws = codes[c]
            nc.vector.quantize_mx(out=wc[:, g, :].bitcast(E5X4), scales=ws[:, g, :],
                                  in_=grouped[s][:].rearrange("p w j -> p (w j)"))

        acc = {}
        prod = {}

        def matmuls(t):
            c, a = t // 4, t % 4
            wc, ws = codes[c]
            ps = psm.tile([P, 512], F32, name="ps", tag="ps")
            for g in range(4):
                nc.tensor.matmul_mx(out=ps[:], lhsT=xq[:, a, g, :].bitcast(E5X4), lhsT_scale=xsc[:, a, g, :],
                                    rhs=wc[:, g, :].bitcast(E5X4), rhs_scale=ws[:, g, :],
                                    start=(g == 0), stop=(g == 3))
            acc[t] = ps

        def products(t):
            a = t % 4
            pab = abp.tile([P, 2, 4, 128], F32, name="pab", tag="pab")
            nc.vector.tensor_tensor(out=pab[:],
                                    in0=acc[t][:].rearrange("p (h d) -> p h d", h=4).unsqueeze(1).to_broadcast([P, 2, 4, 128]),
                                    in1=tabT[:, a].rearrange("p r i e -> p r (i e)").unsqueeze(2).to_broadcast([P, 2, 4, 128]),
                                    op=ALU.mult)
            prod[t] = pab

        def finish(t):
            c, a = t // 4, t % 4
            if a == 0:
                rout[c] = rp.tile([P, 4, 4, 128], F32, name="r", tag="r")
            r = rout[c]
            pab = prod[t]
            eng = nc.vector if (t % 6 == 5 or t == 31) else nc.gpsimd
            eng.tensor_tensor(
                out=r[:, :, a, :].rearrange("p h (i e) -> p h i e", e=2),
                in0=pab[:, 0].rearrange("p h (i e) -> p h i e", e=2),
                in1=pab[:, 1].rearrange("p h (i e) -> p h i e", e=2)[:, :, :, ::-1],
                op=ALU.add,
            )
            h0 = 4 * (c % 4)
            dst = outs[c // 4][0, h0:h0 + 4].rearrange("h (m a) d -> m h a d", a=4)
            if c == 7:
                nc.sync.dma_start(out=dst[:, :, a, :], in_=r[:, :, a, :])
            elif a == 3:
                nc.sync.dma_start(out=dst.rearrange("m h a d -> m h (a d)"), in_=r[:].rearrange("p h a d -> p h (a d)"))

        work = []
        for s in range(32):
            if s in V_UNITS:
                work.append(("I", s))
            work.append(("Q", s))
            if s < 4:
                work.append(("X", s))
        state = {"s": 0, "w": 0, "q": 0, "x": 0, "m": 0}

        def scalar_ahead(upto):
            while state["s"] <= min(upto, 31):
                s = state["s"]
                if s + T_LEAD in T_UNITS:
                    fill(s + T_LEAD)
                if s not in V_UNITS:
                    interleave(s)
                if s == 0:
                    sin_tables()
                if s < 4:
                    x_turn(s)
                state["s"] = s + 1

        def vector_next():
            kind, s = work[state["w"]]
            state["w"] += 1
            if kind == "I":
                interleave(s)
            elif kind == "X":
                x_quantise(s)
                state["x"] += 1
            else:
                quantise(s)
                state["q"] = s + 1
                scalar_ahead(s + 1 + LEAD)

        def tensor_ahead(upto):
            while state["m"] <= min(upto, 31) and 4 * (state["m"] // 4) + 3 < state["q"] and state["x"] > state["m"] % 4:
                matmuls(state["m"])
                state["m"] += 1

        scalar_ahead(LEAD)
        while state["q"] < 4 + A0:
            vector_next()
        for t in range(32):
            tensor_ahead(t + MXLEAD)
            products(t)
            while state["w"] < len(work) and state["q"] < t + 5 + A0:
                vector_next()
            tensor_ahead(t + MXLEAD)
            if t >= 1:
                finish(t - 1)
        finish(31)
